import numpy as np
import ml_dtypes


def mxq(x, axis, fmt="e4m3"):
    dtype, down = {"e4m3": (ml_dtypes.float8_e4m3fn, 7), "e5m2": (ml_dtypes.float8_e5m2, 14)}[fmt]
    v = np.moveaxis(np.asarray(x, np.float32).astype(ml_dtypes.bfloat16).astype(np.float64), axis, -1)
    blocks = v.reshape(v.shape[:-1] + (-1, 32))
    amax = np.abs(blocks).max(-1, keepdims=True)
    byte = np.maximum(np.where(amax > 0, np.frexp(amax)[1] - 1 + 127, 0) - down, 1)
    scale = np.exp2(byte - 127.0)
    codes = (blocks / scale).astype(np.float32).astype(dtype).astype(np.float64)
    return np.moveaxis((codes * scale).reshape(v.shape), -1, axis)


WIDE = False


def mx_kscale(k):
    if not WIDE:
        return np.ones(k)
    levels = np.array([18, -18])
    if k % 512:
        return np.exp2(np.random.permutation(np.resize(levels, k // 32))).repeat(32)
    a = np.empty((k // 512, 16))
    for p in range(k // 512):
        a[p, :8] = np.random.permutation(np.resize(levels, 8))
        for g in range(8):
            far = levels[np.abs(levels - a[p, g]) >= 10]
            a[p, g + 8] = far[np.random.randint(len(far))]
    return np.exp2(a.ravel()).repeat(32)


BF16 = ml_dtypes.bfloat16


def bf(x):
    return np.asarray(x, np.float32).astype(BF16)


def f64(x):
    return np.asarray(x).astype(np.float64)


B, S, D, H = 1, 1024, 768, 6
HD = D // H
HALF = HD // 2
T = B * S


def rope_cache():
    inv_freq = 1.0 / (10000.0 ** (np.arange(HALF) / max(HALF, 1)))
    ang = np.arange(S)[:, None] * inv_freq[None, :]
    return np.cos(ang)[None, None], np.sin(ang)[None, None]


def apply_rope(u, cos, sin):
    u1, u2 = u[..., :HALF], u[..., HALF:]
    return np.concatenate([u1 * cos - u2 * sin, u1 * sin + u2 * cos], axis=-1)


def rope_backward(g, cos, sin):
    g1, g2 = g[..., :HALF], g[..., HALF:]
    return np.concatenate([g1 * cos + g2 * sin, g2 * cos - g1 * sin], axis=-1)


def pair_factors(v):
    v = v.reshape(H, 2, 2, HALF)[:, :, :1]
    return np.concatenate([v, v], axis=2).reshape(H, 2, HD)


def draw_grad(s, u):
    n = np.random.standard_normal((B, H, S, HD))
    e = np.exp2(np.random.randint(-6, 1, (B, 1, S, 1)))
    return bf(n * e / s.reshape(B, 1, S, 1) * u[None, :, None, :])


def setup_inputs():
    s = mx_kscale(T)
    uq = pair_factors(mx_kscale(2 * D))
    uk = pair_factors(mx_kscale(2 * D))
    x0 = bf(np.random.standard_normal((B, S, D)))
    wq0 = bf(np.random.standard_normal((2 * D, D)) / np.sqrt(D))
    bq = bf(np.random.standard_normal(2 * D) * 0.2)
    wk0 = bf(np.random.standard_normal((2 * D, D)) / np.sqrt(D))
    bk = bf(np.random.standard_normal(2 * D) * 0.2)
    g0 = draw_grad(s, uq[:, 0])
    g1 = draw_grad(s, uq[:, 1])
    g2 = draw_grad(s, uk[:, 0])
    g3 = draw_grad(s, uk[:, 1])
    return {"x": bf(f64(x0) * s.reshape(B, S, 1)),
            "Wq": bf(f64(wq0) / uq.reshape(2 * D, 1)),
            "bq": bq,
            "Wk": bf(f64(wk0) / uk.reshape(2 * D, 1)),
            "bk": bk,
            "grad_0": g0, "grad_1": g1, "grad_2": g2, "grad_3": g3}


def reference(x, Wq, bq, Wk, bk, grad_0, grad_1, grad_2, grad_3):
    cos, sin = rope_cache()
    dq = np.concatenate([rope_backward(f64(grad_0), cos, sin), rope_backward(f64(grad_1), cos, sin)], axis=-1)
    dk = np.concatenate([rope_backward(f64(grad_2), cos, sin), rope_backward(f64(grad_3), cos, sin)], axis=-1)
    dq = dq.transpose(0, 2, 1, 3).reshape(T, 2 * D)
    dk = dk.transpose(0, 2, 1, 3).reshape(T, 2 * D)
    dz = np.concatenate([dq, dk], axis=1)
    w = np.concatenate([f64(Wq), f64(Wk)], axis=0)
    dx = mxq(dz, 1, "e5m2") @ mxq(w, 0, "e4m3")
    xt = mxq(f64(x).reshape(T, D), 0, "e4m3")
    dw = mxq(dz, 0, "e5m2").T @ xt
    return dx.reshape(B, S, D), dw[:2 * D], dw[2 * D:]

@@ -1,0 +1,332 @@
+import math
+from contextlib import ExitStack
+
+import concourse.mybir as mybir
+from concourse.masks import make_identity
+
+F32 = mybir.dt.float32
+BF16 = mybir.dt.bfloat16
+I32 = mybir.dt.int32
+U32 = mybir.dt.uint32
+U8 = mybir.dt.uint8
+E4 = mybir.dt.float8_e4m3fn_x4
+E5 = mybir.dt.float8_e5m2_x4
+ALU = mybir.AluOpType
+ACT = mybir.ActivationFunctionType
+
+P = 128
+D = 768
+TOK = 1024
+FEAT = 3072
+NG = 2
+NF = 6
+FLOPS = 2 * 2 * TOK * FEAT * D
+BYTES = 2 * (4 * 6 * TOK * 128 + FEAT * D + TOK * D) + 4 * (TOK * D + FEAT * D)
+
+ORDER = [(0, 0), (0, 1), (1, 0), (1, 1), (2, 0), (2, 1), (3, 0), (3, 1), (4, 0), (4, 1), (5, 0), (5, 1)]
+ROUNDS = [(0, 1, 2), (3, 4, 5)]
+MM_BUDGET = 24
+
+
+def tile_differentialselfattention_pa_v_kernel(
+    tc, x, wq, bq, wk, bk, grad_0, grad_1, grad_2, grad_3, out_0, out_1, out_2
+):
+    nc = tc.nc
+    grads = (grad_0, grad_1, grad_2, grad_3)
+
+    with ExitStack() as ctx:
+        const = ctx.enter_context(tc.tile_pool(name="const", bufs=1))
+        tmp = ctx.enter_context(tc.tile_pool(name="tmp", bufs=2))
+        gpool = ctx.enter_context(tc.tile_pool(name="gpool", bufs=3))
+        rawp = ctx.enter_context(tc.tile_pool(name="rawp", bufs=3))
+        mixp = ctx.enter_context(tc.tile_pool(name="mixp", bufs=2))
+        prod = ctx.enter_context(tc.tile_pool(name="prod", bufs=2))
+        dpool = ctx.enter_context(tc.tile_pool(name="dpool", bufs=2))
+        codes = ctx.enter_context(tc.tile_pool(name="codes", bufs=1))
+        tcodes = ctx.enter_context(tc.tile_pool(name="tcodes", bufs=6))
+        outp = ctx.enter_context(tc.tile_pool(name="outp", bufs=2))
+        psum = ctx.enter_context(tc.psum_pool(name="psum", bufs=1))
+        psmx = ctx.enter_context(tc.psum_pool(name="psmx", bufs=2))
+
+        ident = const.tile([P, P], F32, name="ident")
+        make_identity(nc, ident[:])
+
+        def load_grad(f, g):
+            gt = gpool.tile([P, 4, 512], BF16, name="gt")
+            view = gt[:].rearrange("p (h s) w -> p h s w", s=2)
+            h0 = 2 * (f % 3)
+            for s in range(2):
+                src = grads[2 * (f // 3) + s][0, h0 : h0 + 2, 512 * g : 512 * g + 512, :]
+                nc.sync.dma_start(out=view[:, :, s, :], in_=src.rearrange("h (p j) f -> p h (j f)", j=4))
+            return gt
+
+        def load_raw(src):
+            raw = rawp.tile([P, 4, D], BF16, name="raw")
+            nc.sync.dma_start(out=raw[:], in_=src.rearrange("(p j) d -> p j d", j=4))
+            return raw
+
+        def operand_src(name, n):
+            if name == "x":
+                return x[0, 512 * n : 512 * n + 512, :]
+            w = (wq, wk)[n // 3]
+            r = 512 * (n % 3)
+            return w[r : r + 512, :]
+
+        r_i = const.tile([P, 1], I32, name="r_i")
+        nc.gpsimd.iota(r_i[:], pattern=[[0, 1]], base=0, channel_multiplier=1)
+        tok_i = const.tile([P, 256], I32, name="tok_i")
+        nc.gpsimd.iota(tok_i[:], pattern=[[512, 2], [4, 128]], base=0, channel_multiplier=0)
+
+        bits = const.tile([P, 5], I32, name="bits")
+        fac = const.tile([P, 5], F32, name="fac")
+        j_i = const.tile([P, 1], I32, name="j_i")
+        j_f = const.tile([P, 1], F32, name="j_f")
+        ratio = 1.0e-4 ** (1.0 / 64.0)
+        nc.vector.tensor_scalar(out=j_i[:], in0=r_i[:], scalar1=3, scalar2=None, op0=ALU.bitwise_and)
+        for k in range(5):
+            nc.vector.tensor_scalar(
+                out=bits[:, k : k + 1], in0=r_i[:], scalar1=2 + k, scalar2=1,
+                op0=ALU.logical_shift_right, op1=ALU.bitwise_and,
+            )
+        nc.vector.tensor_copy(out=j_f[:], in_=j_i[:])
+        for k in range(5):
+            nc.vector.tensor_scalar(
+                out=fac[:, k : k + 1], in0=bits[:, k : k + 1], scalar1=ratio ** (2**k) - 1.0, scalar2=1.0,
+                op0=ALU.mult, op1=ALU.add,
+            )
+        tok_f = const.tile([P, 256], F32, name="tok_f")
+        nc.vector.tensor_scalar(out=tok_f[:], in0=tok_i[:], scalar1=j_f[:], scalar2=None, op0=ALU.add)
+        fa = const.tile([P, 1], F32, name="fa")
+        fb = const.tile([P, 1], F32, name="fb")
+        freq = const.tile([P, 2], F32, name="freq")
+        nc.vector.tensor_scalar(
+            out=fa[:], in0=fac[:, 0:1], scalar1=fac[:, 1:2], scalar2=fac[:, 2:3], op0=ALU.mult, op1=ALU.mult
+        )
+        nc.vector.tensor_scalar(
+            out=fb[:], in0=fa[:], scalar1=fac[:, 3:4], scalar2=fac[:, 4:5], op0=ALU.mult, op1=ALU.mult
+        )
+        for b in range(2):
+            nc.vector.tensor_scalar(
+                out=freq[:, b : b + 1], in0=fb[:], scalar1=ratio ** (32 * b) / (2.0 * math.pi), scalar2=None,
+                op0=ALU.mult,
+            )
+        turns = tmp.tile([P, 1024], F32, name="tabf")
+        turns_v = turns[:].rearrange("p (c g b q) -> p c g b q", c=2, g=2, b=2)
+        for c in range(2):
+            for b in range(2):
+                nc.vector.tensor_scalar(
+                    out=turns_v[:, c, :, b, :], in0=tok_f[:].rearrange("p (g q) -> p g q", g=2),
+                    scalar1=freq[:, b : b + 1], scalar2=0.25 * (1 - c), op0=ALU.mult, op1=ALU.add,
+                )
+        whole = tmp.tile([P, 1024], I32, name="tabi")
+        nc.vector.tensor_copy(out=whole[:], in_=turns[:])
+        part = tmp.tile([P, 1024], F32, name="tabf")
+        nc.vector.tensor_tensor(out=part[:], in0=turns[:], in1=whole[:], op=ALU.subtract)
+        neg = tmp.tile([P, 1024], F32, name="tabi2")
+        nc.vector.scalar_tensor_tensor(
+            out=neg[:], in0=part[:], scalar=0.5, in1=part[:], op0=ALU.is_gt, op1=ALU.subtract
+        )
+        trig = tmp.tile([P, 1024], F32, name="tabt")
+        nc.scalar.activation(out=trig[:], in_=neg[:], func=ACT.Sin, scale=-2.0 * math.pi)
+        cos_t = psum.tile([P, 512], F32, name="cos_t")
+        sin_t = psum.tile([P, 512], F32, name="sin_t")
+        for c in range(2):
+            for q in range(4):
+                nc.tensor.transpose(
+                    (cos_t, sin_t)[c][:, 128 * q : 128 * q + 128],
+                    trig[:, 512 * c + 128 * q : 512 * c + 128 * q + 128],
+                    ident[:],
+                )
+
+        def table(t, g):
+            return (
+                t[:, 256 * g : 256 * g + 256]
+                .rearrange("p (i j) -> p i j", j=4)
+                .unsqueeze(1)
+                .to_broadcast([P, 4, 64, 4])
+            )
+
+        def products(gt, g):
+            pc = prod.tile([P, 2048], F32, name="pc")
+            ps = prod.tile([P, 2048], F32, name="ps")
+            src = gt[:].rearrange("p s (j f) -> p s f j", j=4)
+            for out, tab, h in ((pc, cos_t, 0), (ps, sin_t, 1), (pc, cos_t, 1), (ps, sin_t, 0)):
+                nc.vector.tensor_tensor(
+                    out=out[:, 1024 * h : 1024 * h + 1024].rearrange("p (s i j) -> p s i j", s=4, j=4),
+                    in0=src[:, :, 64 * h : 64 * h + 64, :],
+                    in1=table(tab, g),
+                    op=ALU.mult,
+                )
+            return pc, ps
+
+        def adds(pc, ps):
+            dz = dpool.tile([P, 2048], BF16, name="dz", align_bytes=64)
+            dst = dz[:].rearrange("p (t s h m j) -> p t s h m j", t=4, s=4, h=2, m=16)
+            c_v = pc[:].rearrange("p (h s m t j) -> p h t s m j", h=2, s=4, m=16, t=4)
+            s_v = ps[:].rearrange("p (h s m t j) -> p h t s m j", h=2, s=4, m=16, t=4)
+            nc.gpsimd.tensor_tensor(out=dst[:, :, :, 0], in0=c_v[:, 0], in1=s_v[:, 1], op=ALU.add)
+            nc.gpsimd.tensor_tensor(out=dst[:, :, :, 1], in0=c_v[:, 1], in1=s_v[:, 0], op=ALU.subtract)
+            return dz
+
+        def turn(dz):
+            words = dz[:].bitcast(F32).rearrange("p (t m u) -> p t m u", t=4, u=2)
+            banks = []
+            for u in range(2):
+                bank = psum.tile([P, 512], F32, name="turn%d" % u)
+                for t in range(4):
+                    nc.tensor.transpose(bank[:, 128 * t : 128 * t + 128], words[:, t, :, u], ident[:])
+                banks.append(bank)
+            return banks
+
+        def unturn(banks):
+            df = dpool.tile([P, 2048], BF16, name="df", align_bytes=64)
+            dst = df[:].rearrange("p (u e q t) -> p u e q t", u=2, e=2, t=4)
+            for u in range(2):
+                nc.scalar.copy(
+                    out=dst[:, u], in_=banks[u][:].bitcast(BF16).rearrange("p (t q e) -> p e q t", t=4, e=2)
+                )
+            return df
+
+        def quant_dz(pool, src, name):
+            q = pool.tile([P, 512], U32, name=name, align_bytes=64)
+            s = pool.tile([P, 512], U8, name=name + "_s", align_bytes=64)
+            nc.vector.quantize_mx(out=q[:].bitcast(E5), scales=s[:], in_=src[:])
+            return q, s
+
+        def mix(raw):
+            m = mixp.tile([P, 4 * D], BF16, name="mix", align_bytes=64)
+            nc.scalar.copy(
+                out=m[:].rearrange("p (c i t) -> p c t i", i=4, t=4),
+                in_=raw[:].rearrange("p t (c i) -> p c t i", i=4),
+            )
+            return m
+
+        def quant_op(m, name):
+            q = codes.tile([P, D], U32, name=name, align_bytes=64)
+            s = codes.tile([P, D], U8, name=name + "_s", align_bytes=64)
+            for lo, hi in ((0, 512), (512, 768)):
+                nc.vector.quantize_mx(
+                    out=q[:, lo:hi].bitcast(E4), scales=s[:, lo:hi], in_=m[:, 4 * lo : 4 * hi]
+                )
+            return q, s
+
+        tok_q = {}
+        feat_q = {}
+        op_q = {}
+
+        def product(stat, mov, col):
+            banks = []
+            for c, lo in enumerate((0, 256)):
+                bank = psmx.tile([P, 512], F32, name="mx%d" % c)
+                for n, (s, m) in enumerate(zip(stat, mov)):
+                    nc.tensor.matmul_mx(
+                        out=bank[:],
+                        lhsT=s[0][:, col : col + 128].bitcast(E5),
+                        lhsT_scale=s[1][:, col : col + 128],
+                        rhs=m[0][:, lo : lo + 512].bitcast(E4),
+                        rhs_scale=m[1][:, lo : lo + 512],
+                        start=(n == 0),
+                        stop=(n == len(stat) - 1),
+                    )
+                banks.append(bank)
+            return banks
+
+        stage = {}
+
+        def dw_item(f, t):
+            if t % 2 == 0:
+                stage[f, t // 2] = outp.tile([P, 2, D], F32, name="dwo")
+            o = stage[f, t // 2]
+            a, b = product([tok_q[f, 0], tok_q[f, 1]], [op_q["x", 0], op_q["x", 1]], 128 * t)
+            nc.scalar.copy(out=o[:, t % 2, 0:512], in_=a[:])
+            nc.scalar.copy(out=o[:, t % 2, 512:768], in_=b[:, 256:512])
+            if t % 2 == 1:
+                dst = (out_1, out_2)[f // 3][512 * (f % 3) : 512 * (f % 3) + 512, :]
+                nc.scalar.dma_start(
+                    out=dst.rearrange("(m t) d -> m t d", t=4)[:, t - 1 : t + 1, :], in_=o[:]
+                )
+
+        acc = {}
+        for g in range(NG):
+            acc[g] = const.tile([P, 4, D], F32, name="acc%d" % g)
+
+        def dx_item(g, r, j):
+            fs = ROUNDS[r]
+            a, b = product([feat_q[f, g] for f in fs], [op_q["w", f] for f in fs], 128 * j)
+            o = acc[g]
+            for bank, lo, hi, off in ((a, 0, 512, 0), (b, 512, 768, 256)):
+                src = bank[:, off : off + hi - lo]
+                if r == 0:
+                    nc.scalar.copy(out=o[:, j, lo:hi], in_=src)
+                else:
+                    nc.vector.tensor_tensor(out=o[:, j, lo:hi], in0=src, in1=o[:, j, lo:hi], op=ALU.add)
+            if r == len(ROUNDS) - 1 and j % 2 == 1:
+                nc.sync.dma_start(
+                    out=out_0[0, 512 * g : 512 * g + 512, :].rearrange("(p j) d -> p j d", j=4)[:, j - 1 : j + 1, :],
+                    in_=o[:, j - 1 : j + 1, :],
+                )
+
+        n_units = len(ORDER)
+        operands = [("x", 0), ("x", 1)] + [("w", f) for f in range(NF)]
+        gts = {}
+        raws = {}
+        mixes = {}
+
+        def prefetch(k):
+            if k < n_units:
+                gts[k] = load_grad(*ORDER[k])
+            if k < len(operands):
+                raws[k] = load_raw(operand_src(*operands[k]))
+
+        queue = []
+        done_feat = set()
+        done_tok = set()
+        pcs = {}
+        dzs = {}
+        dfs = {}
+        rounds_left = [(g, r) for r in range(len(ROUNDS)) for g in range(NG)]
+        dws_left = list(range(NF))
+
+        def refill():
+            for f in list(dws_left):
+                if (f, 0) in done_tok and (f, 1) in done_tok and ("x", 1) in op_q:
+                    dws_left.remove(f)
+                    queue.extend([(4, dw_item, (f, t)) for t in range(4)])
+            for g, r in list(rounds_left):
+                if all((f, g) in done_feat and ("w", f) in op_q for f in ROUNDS[r]):
+                    rounds_left.remove((g, r))
+                    queue.extend([(2 * len(ROUNDS[r]), dx_item, (g, r, j)) for j in range(4)])
+
+        with tc.manual_schedule():
+            prefetch(0)
+            prefetch(1)
+            k = 0
+            while k < n_units + 3 or queue or rounds_left or dws_left:
+                prefetch(k + 2)
+                if k < len(operands):
+                    mixes[k] = mix(raws.pop(k))
+                if k < n_units:
+                    pcs[k] = products(gts.pop(k), ORDER[k][1])
+                budget = MM_BUDGET
+                while queue and budget > 0:
+                    cost, fn, args = queue.pop(0)
+                    fn(*args)
+                    budget -= cost
+                if 1 <= k <= n_units:
+                    banks = turn(dzs[k - 1])
+                if k < n_units:
+                    dzs[k] = adds(*pcs.pop(k))
+                if 1 <= k <= n_units:
+                    tok_q[ORDER[k - 1]] = quant_dz(tcodes, dzs.pop(k - 1), "tq")
+                    done_tok.add(ORDER[k - 1])
+                if 2 <= k <= n_units + 1:
+                    f, g = ORDER[k - 2]
+                    feat_q[f, g] = quant_dz(codes, dfs.pop(k - 2), "fq%d_%d" % (f, g))
+                    done_feat.add((f, g))
+                if 1 <= k <= n_units:
+                    dfs[k - 1] = unturn(banks)
+                if 1 <= k <= len(operands):
+                    name = operands[k - 1]
+                    op_q[name] = quant_op(mixes.pop(k - 1), "%s%d" % name)
+                refill()
+                k += 1

@@ -23,9 +23,19 @@ NF = 6
 FLOPS = 2 * 2 * TOK * FEAT * D
 BYTES = 2 * (4 * 6 * TOK * 128 + FEAT * D + TOK * D) + 4 * (TOK * D + FEAT * D)
 
-ORDER = [(0, 0), (0, 1), (1, 0), (1, 1), (2, 0), (2, 1), (3, 0), (3, 1), (4, 0), (4, 1), (5, 0), (5, 1)]
-ROUNDS = [(0, 1, 2), (3, 4, 5)]
-MM_BUDGET = 24
+ORDER = [(f, g) for f in range(6) for g in range(2)]
+ROUNDS = {0: [(0, 1, 2), (3, 4, 5)], 1: [(0, 1, 2), (3, 4, 5)]}
+MIX_AT = {1: 0, 2: 1, 3: 2, 4: 3, 5: 4, 6: 5, 7: 6}
+MIXED_BEFORE = [0, 1, 2, 3, 4, 5, 6, 7, 8, 8, 8, 8]
+LOADS = ["o0", "g0", "o1", "g1", "o2", "g2", "o3", "g3", "o4", "g4", "o5", "g5", "o6", "g6", "o7", "g7", "g8", "g9", "g10", "g11"]
+MM_BUDGET = 16
+PIECES = 4
+LAG_T, LAG_F = 2, 3
+N_FIRST = 5
+SYNC = True
+FOLD = False
+TAIL_B = 2
+TAIL_A = 4
 
 
 def tile_differentialselfattention_pa_v_kernel(
@@ -36,7 +46,7 @@ def tile_differentialselfattention_pa_v_kernel(
 
     with ExitStack() as ctx:
         const = ctx.enter_context(tc.tile_pool(name="const", bufs=1))
-        tmp = ctx.enter_context(tc.tile_pool(name="tmp", bufs=2))
+        tmp = ctx.enter_context(tc.tile_pool(name="tmp", bufs=1))
         gpool = ctx.enter_context(tc.tile_pool(name="gpool", bufs=3))
         rawp = ctx.enter_context(tc.tile_pool(name="rawp", bufs=3))
         mixp = ctx.enter_context(tc.tile_pool(name="mixp", bufs=2))
@@ -44,7 +54,7 @@ def tile_differentialselfattention_pa_v_kernel(
         dpool = ctx.enter_context(tc.tile_pool(name="dpool", bufs=2))
         codes = ctx.enter_context(tc.tile_pool(name="codes", bufs=1))
         tcodes = ctx.enter_context(tc.tile_pool(name="tcodes", bufs=6))
-        outp = ctx.enter_context(tc.tile_pool(name="outp", bufs=2))
+        outp = ctx.enter_context(tc.tile_pool(name="outp", bufs=6))
         psum = ctx.enter_context(tc.psum_pool(name="psum", bufs=1))
         psmx = ctx.enter_context(tc.psum_pool(name="psmx", bufs=2))
 
@@ -71,6 +81,9 @@ def tile_differentialselfattention_pa_v_kernel(
             w = (wq, wk)[n // 3]
             r = 512 * (n % 3)
             return w[r : r + 512, :]
+
+        cos_t = psum.tile([P, 512], F32, name="cos_t")
+        sin_t = psum.tile([P, 512], F32, name="sin_t")
 
         r_i = const.tile([P, 1], I32, name="r_i")
         nc.gpsimd.iota(r_i[:], pattern=[[0, 1]], base=0, channel_multiplier=1)
@@ -110,62 +123,60 @@ def tile_differentialselfattention_pa_v_kernel(
                 out=freq[:, b : b + 1], in0=fb[:], scalar1=ratio ** (32 * b) / (2.0 * math.pi), scalar2=None,
                 op0=ALU.mult,
             )
-        turns = tmp.tile([P, 1024], F32, name="tabf")
-        turns_v = turns[:].rearrange("p (c g b q) -> p c g b q", c=2, g=2, b=2)
-        for c in range(2):
-            for b in range(2):
-                nc.vector.tensor_scalar(
-                    out=turns_v[:, c, :, b, :], in0=tok_f[:].rearrange("p (g q) -> p g q", g=2),
-                    scalar1=freq[:, b : b + 1], scalar2=0.25 * (1 - c), op0=ALU.mult, op1=ALU.add,
-                )
-        whole = tmp.tile([P, 1024], I32, name="tabi")
-        nc.vector.tensor_copy(out=whole[:], in_=turns[:])
-        part = tmp.tile([P, 1024], F32, name="tabf")
-        nc.vector.tensor_tensor(out=part[:], in0=turns[:], in1=whole[:], op=ALU.subtract)
-        neg = tmp.tile([P, 1024], F32, name="tabi2")
-        nc.vector.scalar_tensor_tensor(
-            out=neg[:], in0=part[:], scalar=0.5, in1=part[:], op0=ALU.is_gt, op1=ALU.subtract
-        )
-        trig = tmp.tile([P, 1024], F32, name="tabt")
-        nc.scalar.activation(out=trig[:], in_=neg[:], func=ACT.Sin, scale=-2.0 * math.pi)
-        cos_t = psum.tile([P, 512], F32, name="cos_t")
-        sin_t = psum.tile([P, 512], F32, name="sin_t")
-        for c in range(2):
-            for q in range(4):
-                nc.tensor.transpose(
-                    (cos_t, sin_t)[c][:, 128 * q : 128 * q + 128],
-                    trig[:, 512 * c + 128 * q : 512 * c + 128 * q + 128],
-                    ident[:],
-                )
+
+        trig = tmp.tile([P, 1024], F32, name="trig")
+        whole = tmp.tile([P, 1024], I32, name="whole")
+
+        def make_phase(g):
+            v = trig[:, 512 * g : 512 * g + 512]
+            for c in range(2):
+                for b in range(2):
+                    nc.vector.tensor_scalar(
+                        out=v[:, 256 * c + 128 * b : 256 * c + 128 * b + 128], in0=tok_f[:, 128 * g : 128 * g + 128],
+                        scalar1=freq[:, b : b + 1], scalar2=0.25 * (1 - c), op0=ALU.mult, op1=ALU.add,
+                    )
+            n = whole[:, 512 * g : 512 * g + 512]
+            nc.vector.tensor_copy(out=n, in_=v)
+            nc.vector.tensor_tensor(out=v, in0=v, in1=n, op=ALU.subtract)
+            if FOLD:
+                nc.vector.scalar_tensor_tensor(out=v, in0=v, scalar=0.5, in1=v, op0=ALU.is_gt, op1=ALU.subtract)
+
+        def make_trig(g):
+            v = trig[:, 512 * g : 512 * g + 512]
+            nc.scalar.activation(out=v, in_=v, func=ACT.Sin, scale=(-2.0 if FOLD else 2.0) * math.pi)
+            for c in range(2):
+                for b in range(2):
+                    nc.tensor.transpose(
+                        (cos_t, sin_t)[c][:, 256 * g + 128 * b : 256 * g + 128 * b + 128],
+                        v[:, 256 * c + 128 * b : 256 * c + 128 * b + 128],
+                        ident[:],
+                    )
 
         def table(t, g):
             return (
                 t[:, 256 * g : 256 * g + 256]
-                .rearrange("p (i j) -> p i j", j=4)
-                .unsqueeze(1)
-                .to_broadcast([P, 4, 64, 4])
+                .rearrange("p (i j) -> p j i", j=4)
+                .unsqueeze(2)
+                .to_broadcast([P, 4, 4, 64])
             )
 
-        def products(gt, g):
-            pc = prod.tile([P, 2048], F32, name="pc")
-            ps = prod.tile([P, 2048], F32, name="ps")
-            src = gt[:].rearrange("p s (j f) -> p s f j", j=4)
-            for out, tab, h in ((pc, cos_t, 0), (ps, sin_t, 1), (pc, cos_t, 1), (ps, sin_t, 0)):
-                nc.vector.tensor_tensor(
-                    out=out[:, 1024 * h : 1024 * h + 1024].rearrange("p (s i j) -> p s i j", s=4, j=4),
-                    in0=src[:, :, 64 * h : 64 * h + 64, :],
-                    in1=table(tab, g),
-                    op=ALU.mult,
-                )
-            return pc, ps
+        def product_part(gt, g, pc, ps, n):
+            src = gt[:].rearrange("p s (j f) -> p j s f", j=4)
+            out, tab, h = ((pc, cos_t, 0), (ps, sin_t, 1), (pc, cos_t, 1), (ps, sin_t, 0))[n]
+            nc.vector.tensor_tensor(
+                out=out[:, 1024 * h : 1024 * h + 1024].rearrange("p (j s i) -> p j s i", j=4, s=4),
+                in0=src[:, :, :, 64 * h : 64 * h + 64],
+                in1=table(tab, g),
+                op=ALU.mult,
+            )
 
-        def adds(pc, ps):
+        def adds(pc, ps, eng):
             dz = dpool.tile([P, 2048], BF16, name="dz", align_bytes=64)
-            dst = dz[:].rearrange("p (t s h m j) -> p t s h m j", t=4, s=4, h=2, m=16)
-            c_v = pc[:].rearrange("p (h s m t j) -> p h t s m j", h=2, s=4, m=16, t=4)
-            s_v = ps[:].rearrange("p (h s m t j) -> p h t s m j", h=2, s=4, m=16, t=4)
-            nc.gpsimd.tensor_tensor(out=dst[:, :, :, 0], in0=c_v[:, 0], in1=s_v[:, 1], op=ALU.add)
-            nc.gpsimd.tensor_tensor(out=dst[:, :, :, 1], in0=c_v[:, 1], in1=s_v[:, 0], op=ALU.subtract)
+            dst = dz[:].rearrange("p (t s h m j) -> p h s m j t", t=4, s=4, h=2, m=16)
+            c_v = pc[:].rearrange("p (h j s m t) -> p h s m j t", h=2, j=4, s=4, m=16)
+            s_v = ps[:].rearrange("p (h j s m t) -> p h s m j t", h=2, j=4, s=4, m=16)
+            eng.tensor_tensor(out=dst[:, 0], in0=c_v[:, 0], in1=s_v[:, 1], op=ALU.add)
+            eng.tensor_tensor(out=dst[:, 1], in0=c_v[:, 1], in1=s_v[:, 0], op=ALU.subtract)
             return dz
 
         def turn(dz):
@@ -178,11 +189,11 @@ def tile_differentialselfattention_pa_v_kernel(
                 banks.append(bank)
             return banks
 
-        def unturn(banks):
+        def unturn(banks, both=False):
             df = dpool.tile([P, 2048], BF16, name="df", align_bytes=64)
             dst = df[:].rearrange("p (u e q t) -> p u e q t", u=2, e=2, t=4)
             for u in range(2):
-                nc.scalar.copy(
+                (nc.vector.tensor_copy if both and u else nc.scalar.copy)(
                     out=dst[:, u], in_=banks[u][:].bitcast(BF16).rearrange("p (t q e) -> p e q t", t=4, e=2)
                 )
             return df
@@ -193,13 +204,11 @@ def tile_differentialselfattention_pa_v_kernel(
             nc.vector.quantize_mx(out=q[:].bitcast(E5), scales=s[:], in_=src[:])
             return q, s
 
-        def mix(raw):
-            m = mixp.tile([P, 4 * D], BF16, name="mix", align_bytes=64)
-            nc.scalar.copy(
-                out=m[:].rearrange("p (c i t) -> p c t i", i=4, t=4),
-                in_=raw[:].rearrange("p t (c i) -> p c t i", i=4),
+        def mix(raw, m, lo, hi, copy):
+            copy(
+                out=m[:, 4 * lo : 4 * hi].rearrange("p (c i t) -> p c t i", i=4, t=4),
+                in_=raw[:, :, lo:hi].rearrange("p t (c i) -> p c t i", i=4),
             )
-            return m
 
         def quant_op(m, name):
             q = codes.tile([P, D], U32, name=name, align_bytes=64)
@@ -234,58 +243,73 @@ def tile_differentialselfattention_pa_v_kernel(
         stage = {}
 
         def dw_item(f, t):
-            if t % 2 == 0:
-                stage[f, t // 2] = outp.tile([P, 2, D], F32, name="dwo")
-            o = stage[f, t // 2]
+            o = outp.tile([P, D], F32, name="dwo")
             a, b = product([tok_q[f, 0], tok_q[f, 1]], [op_q["x", 0], op_q["x", 1]], 128 * t)
-            nc.scalar.copy(out=o[:, t % 2, 0:512], in_=a[:])
-            nc.scalar.copy(out=o[:, t % 2, 512:768], in_=b[:, 256:512])
-            if t % 2 == 1:
+
+            def scalar_part():
+                nc.scalar.copy(out=o[:, 0:512], in_=a[:])
+                if not late:
+                    nc.scalar.copy(out=o[:, 512:768], in_=b[:, 256:512])
+                    store(nc.scalar)
+
+            def store(eng):
                 dst = (out_1, out_2)[f // 3][512 * (f % 3) : 512 * (f % 3) + 512, :]
-                nc.scalar.dma_start(
-                    out=dst.rearrange("(m t) d -> m t d", t=4)[:, t - 1 : t + 1, :], in_=o[:]
-                )
+                eng.dma_start(out=dst.rearrange("(m t) d -> m t d", t=4)[:, t, :], in_=o[:])
+
+            def vector_part():
+                if late:
+                    nc.vector.tensor_copy(out=o[:, 512:768], in_=b[:, 256:512])
+                    store(nc.sync)
+
+            return vector_part, scalar_part
 
         acc = {}
         for g in range(NG):
             acc[g] = const.tile([P, 4, D], F32, name="acc%d" % g)
 
         def dx_item(g, r, j):
-            fs = ROUNDS[r]
+            fs = ROUNDS[g][r]
             a, b = product([feat_q[f, g] for f in fs], [op_q["w", f] for f in fs], 128 * j)
             o = acc[g]
-            for bank, lo, hi, off in ((a, 0, 512, 0), (b, 512, 768, 256)):
-                src = bank[:, off : off + hi - lo]
+            parts = ((a, 0, 512, 0), (b, 512, 768, 256))
+
+            def scalar_part():
                 if r == 0:
-                    nc.scalar.copy(out=o[:, j, lo:hi], in_=src)
-                else:
-                    nc.vector.tensor_tensor(out=o[:, j, lo:hi], in0=src, in1=o[:, j, lo:hi], op=ALU.add)
-            if r == len(ROUNDS) - 1 and j % 2 == 1:
-                nc.sync.dma_start(
-                    out=out_0[0, 512 * g : 512 * g + 512, :].rearrange("(p j) d -> p j d", j=4)[:, j - 1 : j + 1, :],
-                    in_=o[:, j - 1 : j + 1, :],
-                )
+                    for bank, lo, hi, off in parts:
+                        nc.scalar.copy(out=o[:, j, lo:hi], in_=bank[:, off : off + hi - lo])
+
+            def vector_part():
+                if r > 0:
+                    for bank, lo, hi, off in parts:
+                        nc.vector.tensor_tensor(
+                            out=o[:, j, lo:hi], in0=bank[:, off : off + hi - lo], in1=o[:, j, lo:hi], op=ALU.add
+                        )
+                if r == len(ROUNDS[g]) - 1 and j % 2 == 1:
+                    nc.sync.dma_start(
+                        out=out_0[0, 512 * g : 512 * g + 512, :].rearrange("(p j) d -> p j d", j=4)[
+                            :, j - 1 : j + 1, :
+                        ],
+                        in_=o[:, j - 1 : j + 1, :],
+                    )
+
+            return vector_part, scalar_part
 
         n_units = len(ORDER)
+        last = n_units - 1
         operands = [("x", 0), ("x", 1)] + [("w", f) for f in range(NF)]
         gts = {}
         raws = {}
         mixes = {}
-
-        def prefetch(k):
-            if k < n_units:
-                gts[k] = load_grad(*ORDER[k])
-            if k < len(operands):
-                raws[k] = load_raw(operand_src(*operands[k]))
-
         queue = []
         done_feat = set()
         done_tok = set()
         pcs = {}
         dzs = {}
         dfs = {}
-        rounds_left = [(g, r) for r in range(len(ROUNDS)) for g in range(NG)]
+        turned = {}
+        rounds_left = [(g, r) for r in range(3) for g in range(NG) if r < len(ROUNDS[g])]
         dws_left = list(range(NF))
+        sync_tile = const.tile([P, 1], U32, name="sync_tile")
 
         def refill():
             for f in list(dws_left):
@@ -293,40 +317,124 @@ def tile_differentialselfattention_pa_v_kernel(
                     dws_left.remove(f)
                     queue.extend([(4, dw_item, (f, t)) for t in range(4)])
             for g, r in list(rounds_left):
-                if all((f, g) in done_feat and ("w", f) in op_q for f in ROUNDS[r]):
+                if all((f, g) in done_feat and ("w", f) in op_q for f in ROUNDS[g][r]):
                     rounds_left.remove((g, r))
-                    queue.extend([(2 * len(ROUNDS[r]), dx_item, (g, r, j)) for j in range(4)])
+                    queue.extend([(2 * len(ROUNDS[g][r]), dx_item, (g, r, j)) for j in range(4)])
+
+        loads = list(LOADS)
+
+        def load_some(n):
+            for name in loads[:n]:
+                k = int(name[1:])
+                if name[0] == "g":
+                    gts[k] = load_grad(*ORDER[k])
+                else:
+                    raws[k] = load_raw(operand_src(*operands[k]))
+            loads[:n] = []
+
+        def pieces(i, copy, n):
+            m = mixp.tile([P, 4 * D], BF16, name="mix", align_bytes=64)
+            raw = raws.pop(i)
+            w = D // n
+            mixes[i] = m
+            return [(raw, m, w * q, w * q + w, copy) for q in range(n)]
+
+        def feat_quant(u):
+            q = quant_dz(codes, dfs.pop(u), "fq%d_%d" % ORDER[u])
+            feat_q[ORDER[u]] = q
+            done_feat.add(ORDER[u])
+            return q
+
+        def tok_quant(u):
+            q = quant_dz(tcodes, dzs[u], "tq")
+            tok_q[ORDER[u]] = q
+            done_tok.add(ORDER[u])
+            return q
+
+        pending = []
+
+        def run_item():
+            cost, fn, args = queue.pop(0)
+            parts = fn(*args)
+            parts[1]()
+            pending.append(parts[0])
+            return cost
 
         with tc.manual_schedule():
-            prefetch(0)
-            prefetch(1)
-            k = 0
-            while k < n_units + 3 or queue or rounds_left or dws_left:
-                prefetch(k + 2)
-                if k < len(operands):
-                    mixes[k] = mix(raws.pop(k))
-                if k < n_units:
-                    pcs[k] = products(gts.pop(k), ORDER[k][1])
-                budget = MM_BUDGET
-                while queue and budget > 0:
-                    cost, fn, args = queue.pop(0)
-                    fn(*args)
-                    budget -= cost
-                if 1 <= k <= n_units:
-                    banks = turn(dzs[k - 1])
-                if k < n_units:
-                    dzs[k] = adds(*pcs.pop(k))
-                if 1 <= k <= n_units:
-                    tok_q[ORDER[k - 1]] = quant_dz(tcodes, dzs.pop(k - 1), "tq")
-                    done_tok.add(ORDER[k - 1])
-                if 2 <= k <= n_units + 1:
-                    f, g = ORDER[k - 2]
-                    feat_q[f, g] = quant_dz(codes, dfs.pop(k - 2), "fq%d_%d" % (f, g))
-                    done_feat.add((f, g))
-                if 1 <= k <= n_units:
-                    dfs[k - 1] = unturn(banks)
-                if 1 <= k <= len(operands):
-                    name = operands[k - 1]
-                    op_q[name] = quant_op(mixes.pop(k - 1), "%s%d" % name)
+            late = False
+            load_some(N_FIRST)
+            make_phase(0)
+            fill = pieces(0, nc.scalar.copy, PIECES)
+            mix(*fill.pop(0))
+            mix(*fill.pop(0))
+            make_trig(0)
+            for k in range(n_units):
+                load_some(2)
+                if k == 1:
+                    make_phase(1)
+                    make_trig(1)
+                last_q = None
+                for i in sorted(mixes):
+                    if i < MIXED_BEFORE[k]:
+                        op_q[operands[i]] = last_q = quant_op(mixes.pop(i), "%s%d" % operands[i])
+                if k >= LAG_F:
+                    last_q = feat_quant(k - LAG_F)
+                if k >= LAG_T:
+                    last_q = tok_quant(k - LAG_T)
+                if last_q is not None and SYNC:
+                    nc.gpsimd.tensor_copy(out=sync_tile[:], in_=last_q[0][:, 0:1])
+                if k >= 1:
+                    dzs[k - 1] = adds(*pcs.pop(k - 1), nc.gpsimd)
                 refill()
-                k += 1
+                if k >= 2:
+                    dfs[k - 2] = unturn(turned.pop(k - 2))
+                for i, at in MIX_AT.items():
+                    if at == k:
+                        fill += pieces(i, nc.scalar.copy, PIECES)
+                pcs[k] = (prod.tile([P, 2048], F32, name="pc"), prod.tile([P, 2048], F32, name="ps"))
+                budget = MM_BUDGET
+                n = 0
+                while n < 4 or (queue and budget > 0):
+                    if n < 4:
+                        product_part(gts[k], ORDER[k][1], *pcs[k], n)
+                    while pending:
+                        pending.pop(0)()
+                    if queue and budget > 0:
+                        budget -= run_item()
+                    if fill:
+                        mix(*fill.pop(0))
+                    n += 1
+                while fill:
+                    mix(*fill.pop(0))
+                while pending:
+                    pending.pop(0)()
+                if k >= 1:
+                    turned[k - 1] = turn(dzs[k - 1])
+            late = True
+            dzs[last] = adds(*pcs.pop(last), nc.vector)
+            if last - 2 in dfs:
+                feat_quant(last - 2)
+            refill()
+            for n in range(TAIL_A):
+                if queue:
+                    run_item()
+            dfs[last - 1] = unturn(turned.pop(last - 1), True)
+            tok_quant(last - 1)
+            tok_quant(last)
+            refill()
+            for n in range(TAIL_B):
+                if queue:
+                    run_item()
+            turned[last] = turn(dzs[last])
+            feat_quant(last - 1)
+            while pending:
+                pending.pop(0)()
+            dfs[last] = unturn(turned.pop(last), True)
+            feat_quant(last)
+            refill()
+            while queue:
+                run_item()
+                if len(pending) > 1:
+                    pending.pop(0)()
+            while pending:
+                pending.pop(0)()

@@ -25,17 +25,18 @@ BYTES = 2 * (4 * 6 * TOK * 128 + FEAT * D + TOK * D) + 4 * (TOK * D + FEAT * D)
 
 ORDER = [(f, g) for f in range(6) for g in range(2)]
 ROUNDS = {0: [(0, 1, 2), (3, 4, 5)], 1: [(0, 1, 2), (3, 4, 5)]}
-MIX_AT = {1: 0, 2: 1, 3: 2, 4: 3, 5: 4, 6: 5, 7: 6}
-MIXED_BEFORE = [0, 1, 2, 3, 4, 5, 6, 7, 8, 8, 8, 8]
+MIX_AT = {1: 0, 2: 1, 3: 2, 4: 2, 5: 3, 6: 6, 7: 8}
+MIXED_BEFORE = [0, 1, 3, 4, 5, 6, 6, 6, 7, 7, 8, 8]
 LOADS = ["o0", "g0", "o1", "g1", "o2", "g2", "o3", "g3", "o4", "g4", "o5", "g5", "o6", "g6", "o7", "g7", "g8", "g9", "g10", "g11"]
-MM_BUDGET = 16
-PIECES = 4
+MM_BUDGET = [12, 8, 28, 12, 8, 16, 28, 20, 16, 16, 24, 8]
+PIECES = 6
 LAG_T, LAG_F = 2, 3
 N_FIRST = 5
 SYNC = True
+LATE_FROM = 12
 FOLD = False
 TAIL_B = 2
-TAIL_A = 4
+TAIL_A = 0
 
 
 def tile_differentialselfattention_pa_v_kernel(
@@ -155,28 +156,28 @@ def tile_differentialselfattention_pa_v_kernel(
         def table(t, g):
             return (
                 t[:, 256 * g : 256 * g + 256]
-                .rearrange("p (i j) -> p j i", j=4)
-                .unsqueeze(2)
-                .to_broadcast([P, 4, 4, 64])
+                .rearrange("p (i j) -> p i j", j=4)
+                .unsqueeze(1)
+                .to_broadcast([P, 4, 64, 4])
             )
 
         def product_part(gt, g, pc, ps, n):
-            src = gt[:].rearrange("p s (j f) -> p j s f", j=4)
+            src = gt[:].rearrange("p s (j f) -> p s f j", j=4)
             out, tab, h = ((pc, cos_t, 0), (ps, sin_t, 1), (pc, cos_t, 1), (ps, sin_t, 0))[n]
             nc.vector.tensor_tensor(
-                out=out[:, 1024 * h : 1024 * h + 1024].rearrange("p (j s i) -> p j s i", j=4, s=4),
-                in0=src[:, :, :, 64 * h : 64 * h + 64],
+                out=out[:, 1024 * h : 1024 * h + 1024].rearrange("p (s i j) -> p s i j", s=4, j=4),
+                in0=src[:, :, 64 * h : 64 * h + 64, :],
                 in1=table(tab, g),
                 op=ALU.mult,
             )
 
         def adds(pc, ps, eng):
             dz = dpool.tile([P, 2048], BF16, name="dz", align_bytes=64)
-            dst = dz[:].rearrange("p (t s h m j) -> p h s m j t", t=4, s=4, h=2, m=16)
-            c_v = pc[:].rearrange("p (h j s m t) -> p h s m j t", h=2, j=4, s=4, m=16)
-            s_v = ps[:].rearrange("p (h j s m t) -> p h s m j t", h=2, j=4, s=4, m=16)
-            eng.tensor_tensor(out=dst[:, 0], in0=c_v[:, 0], in1=s_v[:, 1], op=ALU.add)
-            eng.tensor_tensor(out=dst[:, 1], in0=c_v[:, 1], in1=s_v[:, 0], op=ALU.subtract)
+            dst = dz[:].rearrange("p (t s h m j) -> p t s h m j", t=4, s=4, h=2, m=16)
+            c_v = pc[:].rearrange("p (h s m t j) -> p h t s m j", h=2, s=4, m=16, t=4)
+            s_v = ps[:].rearrange("p (h s m t j) -> p h t s m j", h=2, s=4, m=16, t=4)
+            eng.tensor_tensor(out=dst[:, :, :, 0], in0=c_v[:, 0], in1=s_v[:, 1], op=ALU.add)
+            eng.tensor_tensor(out=dst[:, :, :, 1], in0=c_v[:, 1], in1=s_v[:, 0], op=ALU.subtract)
             return dz
 
         def turn(dz):
@@ -369,6 +370,7 @@ def tile_differentialselfattention_pa_v_kernel(
             mix(*fill.pop(0))
             make_trig(0)
             for k in range(n_units):
+                late = k >= LATE_FROM
                 load_some(2)
                 if k == 1:
                     make_phase(1)
@@ -392,7 +394,7 @@ def tile_differentialselfattention_pa_v_kernel(
                     if at == k:
                         fill += pieces(i, nc.scalar.copy, PIECES)
                 pcs[k] = (prod.tile([P, 2048], F32, name="pc"), prod.tile([P, 2048], F32, name="ps"))
-                budget = MM_BUDGET
+                budget = MM_BUDGET[k]
                 n = 0
                 while n < 4 or (queue and budget > 0):
                     if n < 4:

@@ -25,17 +25,18 @@ BYTES = 2 * (4 * 6 * TOK * 128 + FEAT * D + TOK * D) + 4 * (TOK * D + FEAT * D)
 
 ORDER = [(f, g) for f in range(6) for g in range(2)]
 ROUNDS = {0: [(0, 1, 2), (3, 4, 5)], 1: [(0, 1, 2), (3, 4, 5)]}
-MIX_AT = {1: 0, 2: 1, 3: 2, 4: 2, 5: 3, 6: 6, 7: 8}
-MIXED_BEFORE = [0, 1, 3, 4, 5, 6, 6, 6, 7, 7, 8, 8]
-LOADS = ["o0", "g0", "o1", "g1", "o2", "g2", "o3", "g3", "o4", "g4", "o5", "g5", "o6", "g6", "o7", "g7", "g8", "g9", "g10", "g11"]
-MM_BUDGET = [12, 8, 28, 12, 8, 16, 28, 20, 16, 16, 24, 8]
-PIECES = 6
-LAG_T, LAG_F = 2, 3
-N_FIRST = 5
+MIX_AT = {1: 0, 2: 0, 3: 2, 4: 2, 5: 4, 6: 4, 7: 6}
+MIXED_BEFORE = [0, 3, 3, 5, 5, 7, 7, 8, 8, 8, 8, 8]
+LOADS = ["o0", "g0", "o1", "o2", "g1", "o3", "g2", "o4", "g3", "g4", "o5", "g5", "g6", "o6", "g7", "o7", "g8", "g9", "g10", "g11"]
+MM_BUDGET = [24, 28, 8, 16, 16, 24, 16, 16, 16, 16, 20, 16]
+PIECES = 4
+LAG_T, LAG_F = 2, 2
+T_AT = 2
+N_FIRST = 6
 SYNC = True
-LATE_FROM = 12
+LATE_FROM = 10
 FOLD = False
-TAIL_B = 2
+TAIL_B = 0
 TAIL_A = 0
 
 
@@ -153,32 +154,38 @@ def tile_differentialselfattention_pa_v_kernel(
                         ident[:],
                     )
 
-        def table(t, g):
+        def table(t, g, n):
             return (
                 t[:, 256 * g : 256 * g + 256]
                 .rearrange("p (i j) -> p i j", j=4)
                 .unsqueeze(1)
-                .to_broadcast([P, 4, 64, 4])
+                .to_broadcast([P, n, 64, 4])
             )
 
-        def product_part(gt, g, pc, ps, n):
+        def segments(n):
+            w = 8 // n
+            return [(h, s, s + w) for h in range(2) for s in range(0, 4, w)]
+
+        def product_part(gt, g, pc, ps, seg):
+            h, s0, s1 = seg
             src = gt[:].rearrange("p s (j f) -> p s f j", j=4)
-            out, tab, h = ((pc, cos_t, 0), (ps, sin_t, 1), (pc, cos_t, 1), (ps, sin_t, 0))[n]
-            nc.vector.tensor_tensor(
-                out=out[:, 1024 * h : 1024 * h + 1024].rearrange("p (s i j) -> p s i j", s=4, j=4),
-                in0=src[:, :, 64 * h : 64 * h + 64, :],
-                in1=table(tab, g),
-                op=ALU.mult,
-            )
+            for out, tab, hh in ((pc, cos_t, h), (ps, sin_t, 1 - h)):
+                nc.vector.tensor_tensor(
+                    out=out[:, 1024 * hh + 256 * s0 : 1024 * hh + 256 * s1].rearrange("p (s i j) -> p s i j", i=64, j=4),
+                    in0=src[:, s0:s1, 64 * hh : 64 * hh + 64, :],
+                    in1=table(tab, g, s1 - s0),
+                    op=ALU.mult,
+                )
 
-        def adds(pc, ps, eng):
-            dz = dpool.tile([P, 2048], BF16, name="dz", align_bytes=64)
-            dst = dz[:].rearrange("p (t s h m j) -> p t s h m j", t=4, s=4, h=2, m=16)
+        def add_part(pc, ps, dz, eng, seg):
+            h, s0, s1 = seg
+            dst = dz[:].rearrange("p (t s h m j) -> p h t s m j", t=4, s=4, h=2, m=16)
             c_v = pc[:].rearrange("p (h s m t j) -> p h t s m j", h=2, s=4, m=16, t=4)
             s_v = ps[:].rearrange("p (h s m t j) -> p h t s m j", h=2, s=4, m=16, t=4)
-            eng.tensor_tensor(out=dst[:, :, :, 0], in0=c_v[:, 0], in1=s_v[:, 1], op=ALU.add)
-            eng.tensor_tensor(out=dst[:, :, :, 1], in0=c_v[:, 1], in1=s_v[:, 0], op=ALU.subtract)
-            return dz
+            eng.tensor_tensor(
+                out=dst[:, h, :, s0:s1], in0=c_v[:, h, :, s0:s1], in1=s_v[:, 1 - h, :, s0:s1],
+                op=(ALU.add, ALU.subtract)[h],
+            )
 
         def turn(dz):
             words = dz[:].bitcast(F32).rearrange("p (t m u) -> p t m u", t=4, u=2)
@@ -361,6 +368,20 @@ def tile_differentialselfattention_pa_v_kernel(
             pending.append(parts[0])
             return cost
 
+        def op_halves(i):
+            q = codes.tile([P, D], U32, name="%s%d" % operands[i], align_bytes=64)
+            s = codes.tile([P, D], U8, name="%s%d_s" % operands[i], align_bytes=64)
+            m = mixes.pop(i)
+
+            def part(lo, hi):
+                nc.vector.quantize_mx(out=q[:, lo:hi].bitcast(E4), scales=s[:, lo:hi], in_=m[:, 4 * lo : 4 * hi])
+
+            def second():
+                part(512, 768)
+                op_q[operands[i]] = (q, s)
+
+            return [lambda: part(0, 512), second]
+
         with tc.manual_schedule():
             late = False
             load_some(N_FIRST)
@@ -369,36 +390,50 @@ def tile_differentialselfattention_pa_v_kernel(
             mix(*fill.pop(0))
             mix(*fill.pop(0))
             make_trig(0)
+            make_phase(1)
+            make_trig(1)
+            ops = []
+            n_mixed = 0
             for k in range(n_units):
-                late = k >= LATE_FROM
                 load_some(2)
-                if k == 1:
-                    make_phase(1)
-                    make_trig(1)
-                last_q = None
-                for i in sorted(mixes):
-                    if i < MIXED_BEFORE[k]:
-                        op_q[operands[i]] = last_q = quant_op(mixes.pop(i), "%s%d" % operands[i])
-                if k >= LAG_F:
-                    last_q = feat_quant(k - LAG_F)
-                if k >= LAG_T:
-                    last_q = tok_quant(k - LAG_T)
-                if last_q is not None and SYNC:
-                    nc.gpsimd.tensor_copy(out=sync_tile[:], in_=last_q[0][:, 0:1])
-                if k >= 1:
-                    dzs[k - 1] = adds(*pcs.pop(k - 1), nc.gpsimd)
-                refill()
+                while n_mixed < MIXED_BEFORE[k]:
+                    ops += op_halves(n_mixed)
+                    n_mixed += 1
+                n_seg = 4 if ops and k >= 1 else 2
+                segs = segments(n_seg)
+                first = []
                 if k >= 2:
-                    dfs[k - 2] = unturn(turned.pop(k - 2))
+                    first.append(lambda u=k - 2: tok_quant(u))
+                second = []
+                if k >= LAG_F:
+                    second.append(lambda u=k - LAG_F: feat_quant(u))
+                gaps = [[] for n in range(n_seg)]
+                gaps[0] += first
+                gaps[n_seg // 2] += second
+                for n in range(n_seg):
+                    if not gaps[n] and ops:
+                        gaps[n].append(ops.pop(0))
+                if k < 1:
+                    while ops:
+                        ops.pop(0)()
                 for i, at in MIX_AT.items():
                     if at == k:
                         fill += pieces(i, nc.scalar.copy, PIECES)
                 pcs[k] = (prod.tile([P, 2048], F32, name="pc"), prod.tile([P, 2048], F32, name="ps"))
+                dzs[k] = dpool.tile([P, 2048], BF16, name="dz", align_bytes=64)
                 budget = MM_BUDGET[k]
                 n = 0
-                while n < 4 or (queue and budget > 0):
-                    if n < 4:
-                        product_part(gts[k], ORDER[k][1], *pcs[k], n)
+                while n < n_seg or (queue and budget > 0):
+                    if n < n_seg:
+                        for fn in gaps[n]:
+                            fn()
+                        refill()
+                        product_part(gts[k], ORDER[k][1], *pcs[k], segs[n])
+                        if k < last:
+                            add_part(*pcs[k], dzs[k], nc.gpsimd, segs[n])
+                    if n == T_AT * n_seg // 4 and k >= 1:
+                        turned[k - 1] = turn(dzs[k - 1])
+                        dfs[k - 1] = unturn(turned.pop(k - 1))
                     while pending:
                         pending.pop(0)()
                     if queue and budget > 0:
@@ -410,25 +445,22 @@ def tile_differentialselfattention_pa_v_kernel(
                     mix(*fill.pop(0))
                 while pending:
                     pending.pop(0)()
-                if k >= 1:
-                    turned[k - 1] = turn(dzs[k - 1])
             late = True
-            dzs[last] = adds(*pcs.pop(last), nc.vector)
-            if last - 2 in dfs:
-                feat_quant(last - 2)
+            for seg in segments(2):
+                add_part(*pcs[last], dzs[last], nc.vector, seg)
+            tok_quant(last - 1)
+            tok_quant(last)
             refill()
             for n in range(TAIL_A):
                 if queue:
                     run_item()
-            dfs[last - 1] = unturn(turned.pop(last - 1), True)
-            tok_quant(last - 1)
-            tok_quant(last)
+            for u in sorted(dfs):
+                feat_quant(u)
             refill()
             for n in range(TAIL_B):
                 if queue:
                     run_item()
             turned[last] = turn(dzs[last])
-            feat_quant(last - 1)
             while pending:
                 pending.pop(0)()
             dfs[last] = unturn(turned.pop(last), True)
@@ -440,3 +472,4 @@ def tile_differentialselfattention_pa_v_kernel(
                     pending.pop(0)()
             while pending:
                 pending.pop(0)()
+            assert not rounds_left and not dws_left

import math
from contextlib import ExitStack

import concourse.mybir as mybir
from concourse.masks import make_identity

F32 = mybir.dt.float32
BF16 = mybir.dt.bfloat16
I32 = mybir.dt.int32
U32 = mybir.dt.uint32
U8 = mybir.dt.uint8
E4 = mybir.dt.float8_e4m3fn_x4
E5 = mybir.dt.float8_e5m2_x4
ALU = mybir.AluOpType
ACT = mybir.ActivationFunctionType

P = 128
D = 768
TOK = 1024
FEAT = 3072
NG = 2
NF = 6
FLOPS = 2 * 2 * TOK * FEAT * D
BYTES = 2 * (4 * 6 * TOK * 128 + FEAT * D + TOK * D) + 4 * (TOK * D + FEAT * D)

ORDER = [(f, g) for f in range(6) for g in range(2)]
ROUNDS = {0: [(0, 1, 2), (3, 4, 5)], 1: [(0, 1, 2), (3, 4, 5)]}
MIX_AT = {1: 0, 2: 0, 3: 2, 4: 2, 5: 4, 6: 4, 7: 6}
MIXED_BEFORE = [0, 3, 3, 5, 5, 7, 7, 8, 8, 8, 8, 8]
LOADS = ["o0", "g0", "o1", "o2", "g1", "o3", "g2", "o4", "g3", "g4", "o5", "g5", "g6", "o6", "g7", "o7", "g8", "g9", "g10", "g11"]
MM_BUDGET = [24, 28, 8, 16, 16, 24, 16, 16, 16, 16, 20, 16]
PIECES = 4
LAG_T, LAG_F = 2, 2
T_AT = 2
N_FIRST = 6
SYNC = True
LATE_FROM = 10
FOLD = False
TAIL_B = 0
TAIL_A = 0


def tile_differentialselfattention_pa_v_kernel(
    tc, x, wq, bq, wk, bk, grad_0, grad_1, grad_2, grad_3, out_0, out_1, out_2
):
    nc = tc.nc
    grads = (grad_0, grad_1, grad_2, grad_3)

    with ExitStack() as ctx:
        const = ctx.enter_context(tc.tile_pool(name="const", bufs=1))
        tmp = ctx.enter_context(tc.tile_pool(name="tmp", bufs=1))
        gpool = ctx.enter_context(tc.tile_pool(name="gpool", bufs=3))
        rawp = ctx.enter_context(tc.tile_pool(name="rawp", bufs=3))
        mixp = ctx.enter_context(tc.tile_pool(name="mixp", bufs=2))
        prod = ctx.enter_context(tc.tile_pool(name="prod", bufs=2))
        dpool = ctx.enter_context(tc.tile_pool(name="dpool", bufs=2))
        codes = ctx.enter_context(tc.tile_pool(name="codes", bufs=1))
        tcodes = ctx.enter_context(tc.tile_pool(name="tcodes", bufs=6))
        outp = ctx.enter_context(tc.tile_pool(name="outp", bufs=6))
        psum = ctx.enter_context(tc.psum_pool(name="psum", bufs=1))
        psmx = ctx.enter_context(tc.psum_pool(name="psmx", bufs=2))

        ident = const.tile([P, P], F32, name="ident")
        make_identity(nc, ident[:])

        def load_grad(f, g):
            gt = gpool.tile([P, 4, 512], BF16, name="gt")
            view = gt[:].rearrange("p (h s) w -> p h s w", s=2)
            h0 = 2 * (f % 3)
            for s in range(2):
                src = grads[2 * (f // 3) + s][0, h0 : h0 + 2, 512 * g : 512 * g + 512, :]
                nc.sync.dma_start(out=view[:, :, s, :], in_=src.rearrange("h (p j) f -> p h (j f)", j=4))
            return gt

        def load_raw(src):
            raw = rawp.tile([P, 4, D], BF16, name="raw")
            nc.sync.dma_start(out=raw[:], in_=src.rearrange("(p j) d -> p j d", j=4))
            return raw

        def operand_src(name, n):
            if name == "x":
                return x[0, 512 * n : 512 * n + 512, :]
            w = (wq, wk)[n // 3]
            r = 512 * (n % 3)
            return w[r : r + 512, :]

        cos_t = psum.tile([P, 512], F32, name="cos_t")
        sin_t = psum.tile([P, 512], F32, name="sin_t")

        r_i = const.tile([P, 1], I32, name="r_i")
        nc.gpsimd.iota(r_i[:], pattern=[[0, 1]], base=0, channel_multiplier=1)
        tok_i = const.tile([P, 256], I32, name="tok_i")
        nc.gpsimd.iota(tok_i[:], pattern=[[512, 2], [4, 128]], base=0, channel_multiplier=0)

        bits = const.tile([P, 5], I32, name="bits")
        fac = const.tile([P, 5], F32, name="fac")
        j_i = const.tile([P, 1], I32, name="j_i")
        j_f = const.tile([P, 1], F32, name="j_f")
        ratio = 1.0e-4 ** (1.0 / 64.0)
        nc.vector.tensor_scalar(out=j_i[:], in0=r_i[:], scalar1=3, scalar2=None, op0=ALU.bitwise_and)
        for k in range(5):
            nc.vector.tensor_scalar(
                out=bits[:, k : k + 1], in0=r_i[:], scalar1=2 + k, scalar2=1,
                op0=ALU.logical_shift_right, op1=ALU.bitwise_and,
            )
        nc.vector.tensor_copy(out=j_f[:], in_=j_i[:])
        for k in range(5):
            nc.vector.tensor_scalar(
                out=fac[:, k : k + 1], in0=bits[:, k : k + 1], scalar1=ratio ** (2**k) - 1.0, scalar2=1.0,
                op0=ALU.mult, op1=ALU.add,
            )
        tok_f = const.tile([P, 256], F32, name="tok_f")
        nc.vector.tensor_scalar(out=tok_f[:], in0=tok_i[:], scalar1=j_f[:], scalar2=None, op0=ALU.add)
        fa = const.tile([P, 1], F32, name="fa")
        fb = const.tile([P, 1], F32, name="fb")
        freq = const.tile([P, 2], F32, name="freq")
        nc.vector.tensor_scalar(
            out=fa[:], in0=fac[:, 0:1], scalar1=fac[:, 1:2], scalar2=fac[:, 2:3], op0=ALU.mult, op1=ALU.mult
        )
        nc.vector.tensor_scalar(
            out=fb[:], in0=fa[:], scalar1=fac[:, 3:4], scalar2=fac[:, 4:5], op0=ALU.mult, op1=ALU.mult
        )
        for b in range(2):
            nc.vector.tensor_scalar(
                out=freq[:, b : b + 1], in0=fb[:], scalar1=ratio ** (32 * b) / (2.0 * math.pi), scalar2=None,
                op0=ALU.mult,
            )

        trig = tmp.tile([P, 1024], F32, name="trig")
        whole = tmp.tile([P, 1024], I32, name="whole")

        def make_phase(g):
            v = trig[:, 512 * g : 512 * g + 512]
            for c in range(2):
                for b in range(2):
                    nc.vector.tensor_scalar(
                        out=v[:, 256 * c + 128 * b : 256 * c + 128 * b + 128], in0=tok_f[:, 128 * g : 128 * g + 128],
                        scalar1=freq[:, b : b + 1], scalar2=0.25 * (1 - c), op0=ALU.mult, op1=ALU.add,
                    )
            n = whole[:, 512 * g : 512 * g + 512]
            nc.vector.tensor_copy(out=n, in_=v)
            nc.vector.tensor_tensor(out=v, in0=v, in1=n, op=ALU.subtract)
            if FOLD:
                nc.vector.scalar_tensor_tensor(out=v, in0=v, scalar=0.5, in1=v, op0=ALU.is_gt, op1=ALU.subtract)

        def make_trig(g):
            v = trig[:, 512 * g : 512 * g + 512]
            nc.scalar.activation(out=v, in_=v, func=ACT.Sin, scale=(-2.0 if FOLD else 2.0) * math.pi)
            for c in range(2):
                for b in range(2):
                    nc.tensor.transpose(
                        (cos_t, sin_t)[c][:, 256 * g + 128 * b : 256 * g + 128 * b + 128],
                        v[:, 256 * c + 128 * b : 256 * c + 128 * b + 128],
                        ident[:],
                    )

        def table(t, g, n):
            return (
                t[:, 256 * g : 256 * g + 256]
                .rearrange("p (i j) -> p i j", j=4)
                .unsqueeze(1)
                .to_broadcast([P, n, 64, 4])
            )

        def segments(n):
            w = 8 // n
            return [(h, s, s + w) for h in range(2) for s in range(0, 4, w)]

        def product_part(gt, g, pc, ps, seg):
            h, s0, s1 = seg
            src = gt[:].rearrange("p s (j f) -> p s f j", j=4)
            for out, tab, hh in ((pc, cos_t, h), (ps, sin_t, 1 - h)):
                nc.vector.tensor_tensor(
                    out=out[:, 1024 * hh + 256 * s0 : 1024 * hh + 256 * s1].rearrange("p (s i j) -> p s i j", i=64, j=4),
                    in0=src[:, s0:s1, 64 * hh : 64 * hh + 64, :],
                    in1=table(tab, g, s1 - s0),
                    op=ALU.mult,
                )

        def add_part(pc, ps, dz, eng, seg):
            h, s0, s1 = seg
            dst = dz[:].rearrange("p (t s h m j) -> p h t s m j", t=4, s=4, h=2, m=16)
            c_v = pc[:].rearrange("p (h s m t j) -> p h t s m j", h=2, s=4, m=16, t=4)
            s_v = ps[:].rearrange("p (h s m t j) -> p h t s m j", h=2, s=4, m=16, t=4)
            eng.tensor_tensor(
                out=dst[:, h, :, s0:s1], in0=c_v[:, h, :, s0:s1], in1=s_v[:, 1 - h, :, s0:s1],
                op=(ALU.add, ALU.subtract)[h],
            )

        def turn(dz):
            words = dz[:].bitcast(F32).rearrange("p (t m u) -> p t m u", t=4, u=2)
            banks = []
            for u in range(2):
                bank = psum.tile([P, 512], F32, name="turn%d" % u)
                for t in range(4):
                    nc.tensor.transpose(bank[:, 128 * t : 128 * t + 128], words[:, t, :, u], ident[:])
                banks.append(bank)
            return banks

        def unturn(banks, both=False):
            df = dpool.tile([P, 2048], BF16, name="df", align_bytes=64)
            dst = df[:].rearrange("p (u e q t) -> p u e q t", u=2, e=2, t=4)
            for u in range(2):
                (nc.vector.tensor_copy if both and u else nc.scalar.copy)(
                    out=dst[:, u], in_=banks[u][:].bitcast(BF16).rearrange("p (t q e) -> p e q t", t=4, e=2)
                )
            return df

        def quant_dz(pool, src, name):
            q = pool.tile([P, 512], U32, name=name, align_bytes=64)
            s = pool.tile([P, 512], U8, name=name + "_s", align_bytes=64)
            nc.vector.quantize_mx(out=q[:].bitcast(E5), scales=s[:], in_=src[:])
            return q, s

        def mix(raw, m, lo, hi, copy):
            copy(
                out=m[:, 4 * lo : 4 * hi].rearrange("p (c i t) -> p c t i", i=4, t=4),
                in_=raw[:, :, lo:hi].rearrange("p t (c i) -> p c t i", i=4),
            )

        def quant_op(m, name):
            q = codes.tile([P, D], U32, name=name, align_bytes=64)
            s = codes.tile([P, D], U8, name=name + "_s", align_bytes=64)
            for lo, hi in ((0, 512), (512, 768)):
                nc.vector.quantize_mx(
                    out=q[:, lo:hi].bitcast(E4), scales=s[:, lo:hi], in_=m[:, 4 * lo : 4 * hi]
                )
            return q, s

        tok_q = {}
        feat_q = {}
        op_q = {}

        def product(stat, mov, col):
            banks = []
            for c, lo in enumerate((0, 256)):
                bank = psmx.tile([P, 512], F32, name="mx%d" % c)
                for n, (s, m) in enumerate(zip(stat, mov)):
                    nc.tensor.matmul_mx(
                        out=bank[:],
                        lhsT=s[0][:, col : col + 128].bitcast(E5),
                        lhsT_scale=s[1][:, col : col + 128],
                        rhs=m[0][:, lo : lo + 512].bitcast(E4),
                        rhs_scale=m[1][:, lo : lo + 512],
                        start=(n == 0),
                        stop=(n == len(stat) - 1),
                    )
                banks.append(bank)
            return banks

        stage = {}

        def dw_item(f, t):
            o = outp.tile([P, D], F32, name="dwo")
            a, b = product([tok_q[f, 0], tok_q[f, 1]], [op_q["x", 0], op_q["x", 1]], 128 * t)

            def scalar_part():
                nc.scalar.copy(out=o[:, 0:512], in_=a[:])
                if not late:
                    nc.scalar.copy(out=o[:, 512:768], in_=b[:, 256:512])
                    store(nc.scalar)

            def store(eng):
                dst = (out_1, out_2)[f // 3][512 * (f % 3) : 512 * (f % 3) + 512, :]
                eng.dma_start(out=dst.rearrange("(m t) d -> m t d", t=4)[:, t, :], in_=o[:])

            def vector_part():
                if late:
                    nc.vector.tensor_copy(out=o[:, 512:768], in_=b[:, 256:512])
                    store(nc.sync)

            return vector_part, scalar_part

        acc = {}
        for g in range(NG):
            acc[g] = const.tile([P, 4, D], F32, name="acc%d" % g)

        def dx_item(g, r, j):
            fs = ROUNDS[g][r]
            a, b = product([feat_q[f, g] for f in fs], [op_q["w", f] for f in fs], 128 * j)
            o = acc[g]
            parts = ((a, 0, 512, 0), (b, 512, 768, 256))

            def scalar_part():
                if r == 0:
                    for bank, lo, hi, off in parts:
                        nc.scalar.copy(out=o[:, j, lo:hi], in_=bank[:, off : off + hi - lo])

            def vector_part():
                if r > 0:
                    for bank, lo, hi, off in parts:
                        nc.vector.tensor_tensor(
                            out=o[:, j, lo:hi], in0=bank[:, off : off + hi - lo], in1=o[:, j, lo:hi], op=ALU.add
                        )
                if r == len(ROUNDS[g]) - 1 and j % 2 == 1:
                    nc.sync.dma_start(
                        out=out_0[0, 512 * g : 512 * g + 512, :].rearrange("(p j) d -> p j d", j=4)[
                            :, j - 1 : j + 1, :
                        ],
                        in_=o[:, j - 1 : j + 1, :],
                    )

            return vector_part, scalar_part

        n_units = len(ORDER)
        last = n_units - 1
        operands = [("x", 0), ("x", 1)] + [("w", f) for f in range(NF)]
        gts = {}
        raws = {}
        mixes = {}
        queue = []
        done_feat = set()
        done_tok = set()
        pcs = {}
        dzs = {}
        dfs = {}
        turned = {}
        rounds_left = [(g, r) for r in range(3) for g in range(NG) if r < len(ROUNDS[g])]
        dws_left = list(range(NF))
        sync_tile = const.tile([P, 1], U32, name="sync_tile")

        def refill():
            for f in list(dws_left):
                if (f, 0) in done_tok and (f, 1) in done_tok and ("x", 1) in op_q:
                    dws_left.remove(f)
                    queue.extend([(4, dw_item, (f, t)) for t in range(4)])
            for g, r in list(rounds_left):
                if all((f, g) in done_feat and ("w", f) in op_q for f in ROUNDS[g][r]):
                    rounds_left.remove((g, r))
                    queue.extend([(2 * len(ROUNDS[g][r]), dx_item, (g, r, j)) for j in range(4)])

        loads = list(LOADS)

        def load_some(n):
            for name in loads[:n]:
                k = int(name[1:])
                if name[0] == "g":
                    gts[k] = load_grad(*ORDER[k])
                else:
                    raws[k] = load_raw(operand_src(*operands[k]))
            loads[:n] = []

        def pieces(i, copy, n):
            m = mixp.tile([P, 4 * D], BF16, name="mix", align_bytes=64)
            raw = raws.pop(i)
            w = D // n
            mixes[i] = m
            return [(raw, m, w * q, w * q + w, copy) for q in range(n)]

        def feat_quant(u):
            q = quant_dz(codes, dfs.pop(u), "fq%d_%d" % ORDER[u])
            feat_q[ORDER[u]] = q
            done_feat.add(ORDER[u])
            return q

        def tok_quant(u):
            q = quant_dz(tcodes, dzs[u], "tq")
            tok_q[ORDER[u]] = q
            done_tok.add(ORDER[u])
            return q

        pending = []

        def run_item():
            cost, fn, args = queue.pop(0)
            parts = fn(*args)
            parts[1]()
            pending.append(parts[0])
            return cost

        def op_halves(i):
            q = codes.tile([P, D], U32, name="%s%d" % operands[i], align_bytes=64)
            s = codes.tile([P, D], U8, name="%s%d_s" % operands[i], align_bytes=64)
            m = mixes.pop(i)

            def part(lo, hi):
                nc.vector.quantize_mx(out=q[:, lo:hi].bitcast(E4), scales=s[:, lo:hi], in_=m[:, 4 * lo : 4 * hi])

            def second():
                part(512, 768)
                op_q[operands[i]] = (q, s)

            return [lambda: part(0, 512), second]

        with tc.manual_schedule():
            late = False
            load_some(N_FIRST)
            make_phase(0)
            fill = pieces(0, nc.scalar.copy, PIECES)
            mix(*fill.pop(0))
            mix(*fill.pop(0))
            make_trig(0)
            make_phase(1)
            make_trig(1)
            ops = []
            n_mixed = 0
            for k in range(n_units):
                load_some(2)
                while n_mixed < MIXED_BEFORE[k]:
                    ops += op_halves(n_mixed)
                    n_mixed += 1
                n_seg = 4 if ops and k >= 1 else 2
                segs = segments(n_seg)
                first = []
                if k >= 2:
                    first.append(lambda u=k - 2: tok_quant(u))
                second = []
                if k >= LAG_F:
                    second.append(lambda u=k - LAG_F: feat_quant(u))
                gaps = [[] for n in range(n_seg)]
                gaps[0] += first
                gaps[n_seg // 2] += second
                for n in range(n_seg):
                    if not gaps[n] and ops:
                        gaps[n].append(ops.pop(0))
                if k < 1:
                    while ops:
                        ops.pop(0)()
                for i, at in MIX_AT.items():
                    if at == k:
                        fill += pieces(i, nc.scalar.copy, PIECES)
                pcs[k] = (prod.tile([P, 2048], F32, name="pc"), prod.tile([P, 2048], F32, name="ps"))
                dzs[k] = dpool.tile([P, 2048], BF16, name="dz", align_bytes=64)
                budget = MM_BUDGET[k]
                n = 0
                while n < n_seg or (queue and budget > 0):
                    if n < n_seg:
                        for fn in gaps[n]:
                            fn()
                        refill()
                        product_part(gts[k], ORDER[k][1], *pcs[k], segs[n])
                        if k < last:
                            add_part(*pcs[k], dzs[k], nc.gpsimd, segs[n])
                    if n == T_AT * n_seg // 4 and k >= 1:
                        turned[k - 1] = turn(dzs[k - 1])
                        dfs[k - 1] = unturn(turned.pop(k - 1))
                    while pending:
                        pending.pop(0)()
                    if queue and budget > 0:
                        budget -= run_item()
                    if fill:
                        mix(*fill.pop(0))
                    n += 1
                while fill:
                    mix(*fill.pop(0))
                while pending:
                    pending.pop(0)()
            late = True
            for seg in segments(2):
                add_part(*pcs[last], dzs[last], nc.vector, seg)
            tok_quant(last - 1)
            tok_quant(last)
            refill()
            for n in range(TAIL_A):
                if queue:
                    run_item()
            for u in sorted(dfs):
                feat_quant(u)
            refill()
            for n in range(TAIL_B):
                if queue:
                    run_item()
            turned[last] = turn(dzs[last])
            while pending:
                pending.pop(0)()
            dfs[last] = unturn(turned.pop(last), True)
            feat_quant(last)
            refill()
            while queue:
                run_item()
                if len(pending) > 1:
                    pending.pop(0)()
            while pending:
                pending.pop(0)()
            assert not rounds_left and not dws_left
